import numpy as np
import ml_dtypes

BF16 = ml_dtypes.bfloat16


def bf(x):
    return np.asarray(x, np.float32).astype(BF16)


def f32(x):
    return np.asarray(x, np.float32)


def f64(x):
    return np.asarray(x).astype(np.float64)


def striped(idx):
    return np.tile(idx.reshape(-1, 16).T, (8, 1))


C, S, N, F = 128, 2048, 2048, 512


def setup_inputs():
    return {"embed": f32(np.random.standard_normal((C, S))), "pos": f32(0.5 * np.random.standard_normal((C, N))), "w_in": bf(np.random.standard_normal((C, F)) / np.sqrt(C)), "w_out": bf(np.random.standard_normal((F, C)) / np.sqrt(F)), "offs": striped(np.random.permutation(np.tile(np.arange(S), 2))[:N])}


def reference(embed, pos, w_in, w_out, offs):
    idx = offs[:16].T.reshape(-1)
    x0 = f64(embed)[:, idx] + f64(pos)
    h = np.maximum(f64(w_in).T @ x0, 0.0)
    return f64(w_out).T @ h + x0

@@ -1,0 +1,62 @@
+import concourse.mybir as mybir
+
+F32 = mybir.dt.float32
+BF16 = mybir.dt.bfloat16
+U16 = mybir.dt.uint16
+ADD = mybir.AluOpType.add
+RELU = mybir.ActivationFunctionType.Relu
+
+C = 128
+S = 2048
+N = 2048
+F = 512
+PIECE = 512
+PIECES = N // PIECE
+BLOCKS = F // 128
+
+FLOPS = 2 * N * C * F * 2
+
+
+def tile_singlelayertransformer_kernel(tc, embed, pos, w_in, w_out, offs, out):
+    nc = tc.nc
+    with (
+        tc.tile_pool(name="held", bufs=1) as held,
+        tc.tile_pool(name="work", bufs=PIECES) as work,
+        tc.psum_pool(name="hidden_banks", bufs=6) as hidden_banks,
+        tc.psum_pool(name="out_banks", bufs=2) as out_banks,
+    ):
+        offsets = held.tile([C, N // 16], U16, name="offsets")
+        nc.sync.dma_start(offsets[:], offs)
+        table = held.tile([C, S], F32, name="table")
+        nc.sync.dma_start(table[:, : S // 2], embed[:, : S // 2])
+        nc.scalar.dma_start(table[:, S // 2 :], embed[:, S // 2 :])
+        w_in_sb = held.tile([C, F], BF16, name="w_in_sb")
+        nc.scalar.dma_start(w_in_sb[:], w_in)
+        pos_sb = []
+        for j in range(PIECES):
+            pos_j = held.tile([C, PIECE], F32, name=f"pos{j}")
+            queue = nc.sync if j % 2 == 0 else nc.scalar
+            queue.dma_start(pos_j[:], pos[:, j * PIECE : (j + 1) * PIECE])
+            pos_sb.append(pos_j)
+        w_out_sb = held.tile([128, BLOCKS, C], BF16, name="w_out_sb")
+        nc.scalar.dma_start(w_out_sb[:], w_out.rearrange("(b p) c -> p b c", p=128))
+
+        for j in range(PIECES):
+            x0 = work.tile([C, PIECE], F32, name="x0")
+            picked = table[:].indirect(offsets[:, j * (PIECE // 16) : (j + 1) * (PIECE // 16)])
+            nc.vector.tensor_tensor(x0[:], picked, pos_sb[j][:], ADD)
+            x0_bf = work.tile([C, PIECE], BF16, name="x0_bf")
+            nc.vector.tensor_copy(x0_bf[:], x0[:])
+
+            hidden = work.tile([128, BLOCKS, PIECE], BF16, name="hidden")
+            for b in range(BLOCKS):
+                hidden_ps = hidden_banks.tile([128, PIECE], F32, name="hidden_ps")
+                nc.tensor.matmul(hidden_ps[:], w_in_sb[:, b * 128 : (b + 1) * 128], x0_bf[:], start=True, stop=True)
+                nc.scalar.activation(hidden[:, b, :], hidden_ps[:], RELU)
+
+            out_ps = out_banks.tile([C, PIECE], F32, name="out_ps")
+            for b in range(BLOCKS):
+                nc.tensor.matmul(out_ps[:], w_out_sb[:, b, :], hidden[:, b, :], start=(b == 0), stop=(b == BLOCKS - 1))
+            result = work.tile([C, PIECE], F32, name="result")
+            nc.vector.tensor_tensor(result[:], out_ps[:], x0[:], ADD)
+            nc.sync.dma_start(out[:, j * PIECE : (j + 1) * PIECE], result[:])

@@ -50,7 +50,7 @@ def tile_singlelayertransformer_kernel(tc, embed, pos, w_in, w_out, offs, out):
 
             hidden = work.tile([128, BLOCKS, PIECE], BF16, name="hidden")
             for b in range(BLOCKS):
-                hidden_ps = hidden_banks.tile([128, PIECE], F32, name="hidden_ps")
+                hidden_ps = hidden_banks.tile([128, PIECE], BF16, name="hidden_ps")
                 nc.tensor.matmul(hidden_ps[:], w_in_sb[:, b * 128 : (b + 1) * 128], x0_bf[:], start=True, stop=True)
                 nc.scalar.activation(hidden[:, b, :], hidden_ps[:], RELU)
 

@@ -46,13 +46,16 @@ def tile_singlelayertransformer_kernel(tc, embed, pos, w_in, w_out, offs, out):
             picked = table[:].indirect(offsets[:, j * (PIECE // 16) : (j + 1) * (PIECE // 16)])
             nc.vector.tensor_tensor(x0[:], picked, pos_sb[j][:], ADD)
             x0_bf = work.tile([C, PIECE], BF16, name="x0_bf")
-            nc.vector.tensor_copy(x0_bf[:], x0[:])
+            nc.gpsimd.tensor_copy(x0_bf[:], x0[:])
 
             hidden = work.tile([128, BLOCKS, PIECE], BF16, name="hidden")
             for b in range(BLOCKS):
                 hidden_ps = hidden_banks.tile([128, PIECE], BF16, name="hidden_ps")
                 nc.tensor.matmul(hidden_ps[:], w_in_sb[:, b * 128 : (b + 1) * 128], x0_bf[:], start=True, stop=True)
-                nc.scalar.activation(hidden[:, b, :], hidden_ps[:], RELU)
+                if b < BLOCKS - 1:
+                    nc.scalar.activation(hidden[:, b, :], hidden_ps[:], RELU)
+                else:
+                    nc.vector.tensor_scalar_max(hidden[:, b, :], hidden_ps[:], 0.0)
 
             out_ps = out_banks.tile([C, PIECE], F32, name="out_ps")
             for b in range(BLOCKS):

@@ -10,20 +10,20 @@ C = 128
 S = 2048
 N = 2048
 F = 512
-PIECE = 512
-PIECES = N // PIECE
 BLOCKS = F // 128
+PIECES = (128, 384, 512, 512, 384, 128)
+assert sum(PIECES) == N
 
 FLOPS = 2 * N * C * F * 2
 
 
 def tile_singlelayertransformer_kernel(tc, embed, pos, w_in, w_out, offs, out):
     nc = tc.nc
+    starts = [sum(PIECES[:j]) for j in range(len(PIECES))]
     with (
         tc.tile_pool(name="held", bufs=1) as held,
-        tc.tile_pool(name="work", bufs=PIECES) as work,
-        tc.psum_pool(name="hidden_banks", bufs=6) as hidden_banks,
-        tc.psum_pool(name="out_banks", bufs=2) as out_banks,
+        tc.psum_pool(name="hidden_banks", bufs=5) as hidden_banks,
+        tc.psum_pool(name="out_banks", bufs=3) as out_banks,
     ):
         offsets = held.tile([C, N // 16], U16, name="offsets")
         nc.sync.dma_start(offsets[:], offs)
@@ -33,33 +33,32 @@ def tile_singlelayertransformer_kernel(tc, embed, pos, w_in, w_out, offs, out):
         w_in_sb = held.tile([C, F], BF16, name="w_in_sb")
         nc.scalar.dma_start(w_in_sb[:], w_in)
         pos_sb = []
-        for j in range(PIECES):
-            pos_j = held.tile([C, PIECE], F32, name=f"pos{j}")
+        for j, (start, size) in enumerate(zip(starts, PIECES)):
+            pos_j = held.tile([C, size], F32, name=f"pos{j}")
             queue = nc.sync if j % 2 == 0 else nc.scalar
-            queue.dma_start(pos_j[:], pos[:, j * PIECE : (j + 1) * PIECE])
+            queue.dma_start(pos_j[:], pos[:, start : start + size])
             pos_sb.append(pos_j)
         w_out_sb = held.tile([128, BLOCKS, C], BF16, name="w_out_sb")
         nc.scalar.dma_start(w_out_sb[:], w_out.rearrange("(b p) c -> p b c", p=128))
 
-        for j in range(PIECES):
-            x0 = work.tile([C, PIECE], F32, name="x0")
-            picked = table[:].indirect(offsets[:, j * (PIECE // 16) : (j + 1) * (PIECE // 16)])
+        for j, (start, size) in enumerate(zip(starts, PIECES)):
+            x0 = held.tile([C, size], F32, name=f"x0_{j}")
+            picked = table[:].indirect(offsets[:, start // 16 : (start + size) // 16])
             nc.vector.tensor_tensor(x0[:], picked, pos_sb[j][:], ADD)
-            x0_bf = work.tile([C, PIECE], BF16, name="x0_bf")
-            nc.gpsimd.tensor_copy(x0_bf[:], x0[:])
+            x0_bf = held.tile([C, size], BF16, name=f"x0_bf{j}")
+            nc.vector.tensor_copy(x0_bf[:], x0[:])
 
-            hidden = work.tile([128, BLOCKS, PIECE], BF16, name="hidden")
-            for b in range(BLOCKS):
-                hidden_ps = hidden_banks.tile([128, PIECE], BF16, name="hidden_ps")
-                nc.tensor.matmul(hidden_ps[:], w_in_sb[:, b * 128 : (b + 1) * 128], x0_bf[:], start=True, stop=True)
-                if b < BLOCKS - 1:
-                    nc.scalar.activation(hidden[:, b, :], hidden_ps[:], RELU)
-                else:
-                    nc.vector.tensor_scalar_max(hidden[:, b, :], hidden_ps[:], 0.0)
+            hidden = held.tile([128, BLOCKS, size], BF16, name=f"hidden{j}")
+            for pair in range(BLOCKS // 2):
+                hidden_ps = hidden_banks.tile([128, 2, size], BF16, name="hidden_ps")
+                for half in range(2):
+                    b = 2 * pair + half
+                    nc.tensor.matmul(hidden_ps[:, half, :], w_in_sb[:, b * 128 : (b + 1) * 128], x0_bf[:], start=True, stop=True)
+                nc.scalar.activation(hidden[:, 2 * pair : 2 * pair + 2, :], hidden_ps[:], RELU)
 
-            out_ps = out_banks.tile([C, PIECE], F32, name="out_ps")
+            out_ps = out_banks.tile([C, size], F32, name="out_ps")
             for b in range(BLOCKS):
                 nc.tensor.matmul(out_ps[:], w_out_sb[:, b, :], hidden[:, b, :], start=(b == 0), stop=(b == BLOCKS - 1))
-            result = work.tile([C, PIECE], F32, name="result")
+            result = held.tile([C, size], F32, name=f"result{j}")
             nc.vector.tensor_tensor(result[:], out_ps[:], x0[:], ADD)
-            nc.sync.dma_start(out[:, j * PIECE : (j + 1) * PIECE], result[:])
+            nc.sync.dma_start(out[:, start : start + size], result[:])

@@ -11,15 +11,18 @@ S = 2048
 N = 2048
 F = 512
 BLOCKS = F // 128
-PIECES = (128, 384, 512, 512, 384, 128)
+PIECES = (128, 128, 256, 512, 512, 384, 128)
 assert sum(PIECES) == N
+STARTS = [sum(PIECES[:j]) for j in range(len(PIECES))]
+LOOK = 256
+POS_LOADS = (256, 768, 1024)
+assert sum(POS_LOADS) == N
 
 FLOPS = 2 * N * C * F * 2
 
 
 def tile_singlelayertransformer_kernel(tc, embed, pos, w_in, w_out, offs, out):
     nc = tc.nc
-    starts = [sum(PIECES[:j]) for j in range(len(PIECES))]
     with (
         tc.tile_pool(name="held", bufs=1) as held,
         tc.psum_pool(name="hidden_banks", bufs=5) as hidden_banks,
@@ -32,33 +35,50 @@ def tile_singlelayertransformer_kernel(tc, embed, pos, w_in, w_out, offs, out):
         nc.scalar.dma_start(table[:, S // 2 :], embed[:, S // 2 :])
         w_in_sb = held.tile([C, F], BF16, name="w_in_sb")
         nc.scalar.dma_start(w_in_sb[:], w_in)
-        pos_sb = []
-        for j, (start, size) in enumerate(zip(starts, PIECES)):
-            pos_j = held.tile([C, size], F32, name=f"pos{j}")
-            queue = nc.sync if j % 2 == 0 else nc.scalar
-            queue.dma_start(pos_j[:], pos[:, start : start + size])
-            pos_sb.append(pos_j)
+        pos_sb = held.tile([C, N], F32, name="pos_sb")
+        first = 0
+        for width in POS_LOADS:
+            nc.sync.dma_start(pos_sb[:, first : first + width], pos[:, first : first + width])
+            first += width
         w_out_sb = held.tile([128, BLOCKS, C], BF16, name="w_out_sb")
         nc.scalar.dma_start(w_out_sb[:], w_out.rearrange("(b p) c -> p b c", p=128))
 
-        for j, (start, size) in enumerate(zip(starts, PIECES)):
-            x0 = held.tile([C, size], F32, name=f"x0_{j}")
-            picked = table[:].indirect(offsets[:, start // 16 : (start + size) // 16])
-            nc.vector.tensor_tensor(x0[:], picked, pos_sb[j][:], ADD)
-            x0_bf = held.tile([C, size], BF16, name=f"x0_bf{j}")
-            nc.vector.tensor_copy(x0_bf[:], x0[:])
+        x0 = [held.tile([C, size], F32, name=f"x0_{j}") for j, size in enumerate(PIECES)]
+        x0_bf = [held.tile([C, size], BF16, name=f"x0_bf{j}") for j, size in enumerate(PIECES)]
+        hidden = [held.tile([128, BLOCKS, size], BF16, name=f"hidden{j}") for j, size in enumerate(PIECES)]
 
-            hidden = held.tile([128, BLOCKS, size], BF16, name=f"hidden{j}")
+        def look_up(j):
+            for first in range(0, PIECES[j], LOOK):
+                last = min(first + LOOK, PIECES[j])
+                token = STARTS[j] + first
+                picked = table[:].indirect(offsets[:, token // 16 : (STARTS[j] + last) // 16])
+                nc.vector.tensor_tensor(x0[j][:, first:last], picked, pos_sb[:, token : STARTS[j] + last], ADD)
+                nc.vector.tensor_copy(x0_bf[j][:, first:last], x0[j][:, first:last])
+
+        def hidden_layer(j):
             for pair in range(BLOCKS // 2):
-                hidden_ps = hidden_banks.tile([128, 2, size], BF16, name="hidden_ps")
+                hidden_ps = hidden_banks.tile([128, 2, PIECES[j]], BF16, name="hidden_ps")
                 for half in range(2):
                     b = 2 * pair + half
-                    nc.tensor.matmul(hidden_ps[:, half, :], w_in_sb[:, b * 128 : (b + 1) * 128], x0_bf[:], start=True, stop=True)
-                nc.scalar.activation(hidden[:, 2 * pair : 2 * pair + 2, :], hidden_ps[:], RELU)
+                    nc.tensor.matmul(hidden_ps[:, half, :], w_in_sb[:, b * 128 : (b + 1) * 128], x0_bf[j][:], start=True, stop=True)
+                if pair == 1 and STARTS[j] >= N // 2:
+                    nc.vector.tensor_scalar_max(hidden[j][:, 2 * pair : 2 * pair + 2, :], hidden_ps[:], 0.0)
+                else:
+                    nc.scalar.activation(hidden[j][:, 2 * pair : 2 * pair + 2, :], hidden_ps[:], RELU)
 
+        def output_layer(j):
+            start, size = STARTS[j], PIECES[j]
             out_ps = out_banks.tile([C, size], F32, name="out_ps")
             for b in range(BLOCKS):
-                nc.tensor.matmul(out_ps[:], w_out_sb[:, b, :], hidden[:, b, :], start=(b == 0), stop=(b == BLOCKS - 1))
+                nc.tensor.matmul(out_ps[:], w_out_sb[:, b, :], hidden[j][:, b, :], start=(b == 0), stop=(b == BLOCKS - 1))
             result = held.tile([C, size], F32, name=f"result{j}")
-            nc.vector.tensor_tensor(result[:], out_ps[:], x0[:], ADD)
+            nc.vector.tensor_tensor(result[:], out_ps[:], x0[j][:], ADD)
             nc.sync.dma_start(out[:, start : start + size], result[:])
+
+        for j in range(len(PIECES)):
+            look_up(j)
+        hidden_layer(0)
+        for j in range(len(PIECES)):
+            if j + 1 < len(PIECES):
+                hidden_layer(j + 1)
+            output_layer(j)

@@ -36,10 +36,10 @@ def tile_singlelayertransformer_kernel(tc, embed, pos, w_in, w_out, offs, out):
         w_in_sb = held.tile([C, F], BF16, name="w_in_sb")
         nc.scalar.dma_start(w_in_sb[:], w_in)
         pos_sb = held.tile([C, N], F32, name="pos_sb")
-        first = 0
+        loaded = 0
         for width in POS_LOADS:
-            nc.sync.dma_start(pos_sb[:, first : first + width], pos[:, first : first + width])
-            first += width
+            nc.sync.dma_start(pos_sb[:, loaded : loaded + width], pos[:, loaded : loaded + width])
+            loaded += width
         w_out_sb = held.tile([128, BLOCKS, C], BF16, name="w_out_sb")
         nc.scalar.dma_start(w_out_sb[:], w_out.rearrange("(b p) c -> p b c", p=128))
 
@@ -50,10 +50,13 @@ def tile_singlelayertransformer_kernel(tc, embed, pos, w_in, w_out, offs, out):
         def look_up(j):
             for first in range(0, PIECES[j], LOOK):
                 last = min(first + LOOK, PIECES[j])
-                token = STARTS[j] + first
-                picked = table[:].indirect(offsets[:, token // 16 : (STARTS[j] + last) // 16])
-                nc.vector.tensor_tensor(x0[j][:, first:last], picked, pos_sb[:, token : STARTS[j] + last], ADD)
-                nc.vector.tensor_copy(x0_bf[j][:, first:last], x0[j][:, first:last])
+                lo, hi = STARTS[j] + first, STARTS[j] + last
+                picked = table[:].indirect(offsets[:, lo // 16 : hi // 16])
+                nc.vector.tensor_tensor(x0[j][:, first:last], picked, pos_sb[:, lo:hi], ADD)
+                if STARTS[j] < N // 4:
+                    nc.scalar.copy(x0_bf[j][:, first:last], x0[j][:, first:last])
+                else:
+                    nc.vector.tensor_copy(x0_bf[j][:, first:last], x0[j][:, first:last])
 
         def hidden_layer(j):
             for pair in range(BLOCKS // 2):

@@ -15,7 +15,7 @@ PIECES = (128, 128, 256, 512, 512, 384, 128)
 assert sum(PIECES) == N
 STARTS = [sum(PIECES[:j]) for j in range(len(PIECES))]
 LOOK = 256
-POS_LOADS = (256, 768, 1024)
+POS_LOADS = (256, 256, 512, 1024)
 assert sum(POS_LOADS) == N
 
 FLOPS = 2 * N * C * F * 2
@@ -31,17 +31,18 @@ def tile_singlelayertransformer_kernel(tc, embed, pos, w_in, w_out, offs, out):
         offsets = held.tile([C, N // 16], U16, name="offsets")
         nc.sync.dma_start(offsets[:], offs)
         table = held.tile([C, S], F32, name="table")
-        nc.sync.dma_start(table[:, : S // 2], embed[:, : S // 2])
-        nc.scalar.dma_start(table[:, S // 2 :], embed[:, S // 2 :])
-        w_in_sb = held.tile([C, F], BF16, name="w_in_sb")
-        nc.scalar.dma_start(w_in_sb[:], w_in)
+        nc.sync.dma_start(table[:], embed)
         pos_sb = held.tile([C, N], F32, name="pos_sb")
+        w_in_sb = held.tile([C, F], BF16, name="w_in_sb")
+        w_out_sb = held.tile([128, BLOCKS, C], BF16, name="w_out_sb")
         loaded = 0
-        for width in POS_LOADS:
+        for k, width in enumerate(POS_LOADS):
             nc.sync.dma_start(pos_sb[:, loaded : loaded + width], pos[:, loaded : loaded + width])
             loaded += width
-        w_out_sb = held.tile([128, BLOCKS, C], BF16, name="w_out_sb")
-        nc.scalar.dma_start(w_out_sb[:], w_out.rearrange("(b p) c -> p b c", p=128))
+            if k == 0:
+                nc.sync.dma_start(w_in_sb[:], w_in)
+            if k == 1:
+                nc.sync.dma_start(w_out_sb[:], w_out.rearrange("(b p) c -> p b c", p=128))
 
         x0 = [held.tile([C, size], F32, name=f"x0_{j}") for j, size in enumerate(PIECES)]
         x0_bf = [held.tile([C, size], BF16, name=f"x0_bf{j}") for j, size in enumerate(PIECES)]

@@ -31,7 +31,8 @@ def tile_singlelayertransformer_kernel(tc, embed, pos, w_in, w_out, offs, out):
         offsets = held.tile([C, N // 16], U16, name="offsets")
         nc.sync.dma_start(offsets[:], offs)
         table = held.tile([C, S], F32, name="table")
-        nc.sync.dma_start(table[:], embed)
+        nc.sync.dma_start(table[:, : S // 2], embed[:, : S // 2])
+        nc.scalar.dma_start(table[:, S // 2 :], embed[:, S // 2 :])
         pos_sb = held.tile([C, N], F32, name="pos_sb")
         w_in_sb = held.tile([C, F], BF16, name="w_in_sb")
         w_out_sb = held.tile([128, BLOCKS, C], BF16, name="w_out_sb")

@@ -15,8 +15,9 @@ PIECES = (128, 128, 256, 512, 512, 384, 128)
 assert sum(PIECES) == N
 STARTS = [sum(PIECES[:j]) for j in range(len(PIECES))]
 LOOK = 256
-POS_LOADS = (256, 256, 512, 1024)
+POS_LOADS = (128, 384, 512, 1024)
 assert sum(POS_LOADS) == N
+SPLIT = (S - N // 32 - POS_LOADS[0]) // 2
 
 FLOPS = 2 * N * C * F * 2
 
@@ -31,8 +32,8 @@ def tile_singlelayertransformer_kernel(tc, embed, pos, w_in, w_out, offs, out):
         offsets = held.tile([C, N // 16], U16, name="offsets")
         nc.sync.dma_start(offsets[:], offs)
         table = held.tile([C, S], F32, name="table")
-        nc.sync.dma_start(table[:, : S // 2], embed[:, : S // 2])
-        nc.scalar.dma_start(table[:, S // 2 :], embed[:, S // 2 :])
+        nc.sync.dma_start(table[:, :SPLIT], embed[:, :SPLIT])
+        nc.scalar.dma_start(table[:, SPLIT:], embed[:, SPLIT:])
         pos_sb = held.tile([C, N], F32, name="pos_sb")
         w_in_sb = held.tile([C, F], BF16, name="w_in_sb")
         w_out_sb = held.tile([128, BLOCKS, C], BF16, name="w_out_sb")
@@ -40,9 +41,8 @@ def tile_singlelayertransformer_kernel(tc, embed, pos, w_in, w_out, offs, out):
         for k, width in enumerate(POS_LOADS):
             nc.sync.dma_start(pos_sb[:, loaded : loaded + width], pos[:, loaded : loaded + width])
             loaded += width
-            if k == 0:
-                nc.sync.dma_start(w_in_sb[:], w_in)
             if k == 1:
+                nc.sync.dma_start(w_in_sb[:], w_in)
                 nc.sync.dma_start(w_out_sb[:], w_out.rearrange("(b p) c -> p b c", p=128))
 
         x0 = [held.tile([C, size], F32, name=f"x0_{j}") for j, size in enumerate(PIECES)]

@@ -11,13 +11,17 @@ S = 2048
 N = 2048
 F = 512
 BLOCKS = F // 128
-PIECES = (128, 128, 256, 512, 512, 384, 128)
+PIECES = (64, 64, 128) + 6 * (256,) + (128, 128)
 assert sum(PIECES) == N
 STARTS = [sum(PIECES[:j]) for j in range(len(PIECES))]
+AHEAD = 2
+LOOK_AHEAD = 3
 LOOK = 256
 POS_LOADS = (128, 384, 512, 1024)
 assert sum(POS_LOADS) == N
 SPLIT = (S - N // 32 - POS_LOADS[0]) // 2
+
+WARM_UP = 12
 
 FLOPS = 2 * N * C * F * 2
 
@@ -29,6 +33,12 @@ def tile_singlelayertransformer_kernel(tc, embed, pos, w_in, w_out, offs, out):
         tc.psum_pool(name="hidden_banks", bufs=5) as hidden_banks,
         tc.psum_pool(name="out_banks", bufs=3) as out_banks,
     ):
+        zeros = held.tile([C, 512], BF16, name="zeros")
+        nc.vector.memset(zeros[:], 0.0)
+        warm_ps = hidden_banks.tile([128, 512], F32, name="warm_ps", tag="hidden_ps")
+        for i in range(WARM_UP):
+            nc.tensor.matmul(warm_ps[:], zeros[:, :C], zeros[:], start=True, stop=True)
+
         offsets = held.tile([C, N // 16], U16, name="offsets")
         nc.sync.dma_start(offsets[:], offs)
         table = held.tile([C, S], F32, name="table")
@@ -80,10 +90,10 @@ def tile_singlelayertransformer_kernel(tc, embed, pos, w_in, w_out, offs, out):
             nc.vector.tensor_tensor(result[:], out_ps[:], x0[j][:], ADD)
             nc.sync.dma_start(out[:, start : start + size], result[:])
 
-        for j in range(len(PIECES)):
-            look_up(j)
-        hidden_layer(0)
-        for j in range(len(PIECES)):
-            if j + 1 < len(PIECES):
-                hidden_layer(j + 1)
-            output_layer(j)
+        for i in range(-AHEAD - LOOK_AHEAD, len(PIECES)):
+            if i + AHEAD + LOOK_AHEAD < len(PIECES):
+                look_up(i + AHEAD + LOOK_AHEAD)
+            if 0 <= i + AHEAD < len(PIECES):
+                hidden_layer(i + AHEAD)
+            if i >= 0:
+                output_layer(i)

@@ -11,8 +11,9 @@ S = 2048
 N = 2048
 F = 512
 BLOCKS = F // 128
-PIECES = (64, 64, 128) + 6 * (256,) + (128, 128)
+PIECES = (64, 64, 128, 128, 128) + 5 * (256,) + (128, 128)
 assert sum(PIECES) == N
+HEAD = 512
 STARTS = [sum(PIECES[:j]) for j in range(len(PIECES))]
 AHEAD = 2
 LOOK_AHEAD = 3
@@ -21,7 +22,7 @@ POS_LOADS = (128, 384, 512, 1024)
 assert sum(POS_LOADS) == N
 SPLIT = (S - N // 32 - POS_LOADS[0]) // 2
 
-WARM_UP = 12
+WARM_UP = 11
 
 FLOPS = 2 * N * C * F * 2
 
@@ -53,6 +54,7 @@ def tile_singlelayertransformer_kernel(tc, embed, pos, w_in, w_out, offs, out):
             loaded += width
             if k == 1:
                 nc.sync.dma_start(w_in_sb[:], w_in)
+            if k == 2:
                 nc.sync.dma_start(w_out_sb[:], w_out.rearrange("(b p) c -> p b c", p=128))
 
         x0 = [held.tile([C, size], F32, name=f"x0_{j}") for j, size in enumerate(PIECES)]
@@ -65,21 +67,21 @@ def tile_singlelayertransformer_kernel(tc, embed, pos, w_in, w_out, offs, out):
                 lo, hi = STARTS[j] + first, STARTS[j] + last
                 picked = table[:].indirect(offsets[:, lo // 16 : hi // 16])
                 nc.vector.tensor_tensor(x0[j][:, first:last], picked, pos_sb[:, lo:hi], ADD)
-                if STARTS[j] < N // 4:
+                if STARTS[j] < HEAD:
                     nc.scalar.copy(x0_bf[j][:, first:last], x0[j][:, first:last])
                 else:
                     nc.vector.tensor_copy(x0_bf[j][:, first:last], x0[j][:, first:last])
 
         def hidden_layer(j):
-            for pair in range(BLOCKS // 2):
-                hidden_ps = hidden_banks.tile([128, 2, PIECES[j]], BF16, name="hidden_ps")
-                for half in range(2):
-                    b = 2 * pair + half
-                    nc.tensor.matmul(hidden_ps[:, half, :], w_in_sb[:, b * 128 : (b + 1) * 128], x0_bf[j][:], start=True, stop=True)
-                if pair == 1 and STARTS[j] >= N // 2:
-                    nc.vector.tensor_scalar_max(hidden[j][:, 2 * pair : 2 * pair + 2, :], hidden_ps[:], 0.0)
+            together = BLOCKS if STARTS[j] < HEAD else BLOCKS // 2
+            for first in range(0, BLOCKS, together):
+                hidden_ps = hidden_banks.tile([128, together, PIECES[j]], BF16, name="hidden_ps")
+                for b in range(first, first + together):
+                    nc.tensor.matmul(hidden_ps[:, b - first, :], w_in_sb[:, b * 128 : (b + 1) * 128], x0_bf[j][:], start=True, stop=True)
+                if first > 0 and STARTS[j] >= N // 2:
+                    nc.vector.tensor_scalar_max(hidden[j][:, first : first + together, :], hidden_ps[:], 0.0)
                 else:
-                    nc.scalar.activation(hidden[j][:, 2 * pair : 2 * pair + 2, :], hidden_ps[:], RELU)
+                    nc.scalar.activation(hidden[j][:, first : first + together, :], hidden_ps[:], RELU)
 
         def output_layer(j):
             start, size = STARTS[j], PIECES[j]

@@ -18,7 +18,7 @@ STARTS = [sum(PIECES[:j]) for j in range(len(PIECES))]
 AHEAD = 2
 LOOK_AHEAD = 3
 LOOK = 256
-POS_LOADS = (128, 384, 512, 1024)
+POS_LOADS = (128, 128, 256, 512, 512, 512)
 assert sum(POS_LOADS) == N
 SPLIT = (S - N // 32 - POS_LOADS[0]) // 2
 
@@ -54,7 +54,7 @@ def tile_singlelayertransformer_kernel(tc, embed, pos, w_in, w_out, offs, out):
             loaded += width
             if k == 1:
                 nc.sync.dma_start(w_in_sb[:], w_in)
-            if k == 2:
+            if k == 3:
                 nc.sync.dma_start(w_out_sb[:], w_out.rearrange("(b p) c -> p b c", p=128))
 
         x0 = [held.tile([C, size], F32, name=f"x0_{j}") for j, size in enumerate(PIECES)]

@@ -11,7 +11,7 @@ S = 2048
 N = 2048
 F = 512
 BLOCKS = F // 128
-PIECES = (64, 64, 128, 128, 128) + 5 * (256,) + (128, 128)
+PIECES = (64, 64, 128, 128, 128) + 5 * (256,) + (192, 64)
 assert sum(PIECES) == N
 HEAD = 512
 STARTS = [sum(PIECES[:j]) for j in range(len(PIECES))]

import concourse.mybir as mybir

F32 = mybir.dt.float32
BF16 = mybir.dt.bfloat16
U16 = mybir.dt.uint16
ADD = mybir.AluOpType.add
RELU = mybir.ActivationFunctionType.Relu

C = 128
S = 2048
N = 2048
F = 512
BLOCKS = F // 128
PIECES = (64, 64, 128, 128, 128) + 5 * (256,) + (192, 64)
assert sum(PIECES) == N
HEAD = 512
STARTS = [sum(PIECES[:j]) for j in range(len(PIECES))]
AHEAD = 2
LOOK_AHEAD = 3
LOOK = 256
POS_LOADS = (128, 128, 256, 512, 512, 512)
assert sum(POS_LOADS) == N
SPLIT = (S - N // 32 - POS_LOADS[0]) // 2

WARM_UP = 11

FLOPS = 2 * N * C * F * 2


def tile_singlelayertransformer_kernel(tc, embed, pos, w_in, w_out, offs, out):
    nc = tc.nc
    with (
        tc.tile_pool(name="held", bufs=1) as held,
        tc.psum_pool(name="hidden_banks", bufs=5) as hidden_banks,
        tc.psum_pool(name="out_banks", bufs=3) as out_banks,
    ):
        zeros = held.tile([C, 512], BF16, name="zeros")
        nc.vector.memset(zeros[:], 0.0)
        warm_ps = hidden_banks.tile([128, 512], F32, name="warm_ps", tag="hidden_ps")
        for i in range(WARM_UP):
            nc.tensor.matmul(warm_ps[:], zeros[:, :C], zeros[:], start=True, stop=True)

        offsets = held.tile([C, N // 16], U16, name="offsets")
        nc.sync.dma_start(offsets[:], offs)
        table = held.tile([C, S], F32, name="table")
        nc.sync.dma_start(table[:, :SPLIT], embed[:, :SPLIT])
        nc.scalar.dma_start(table[:, SPLIT:], embed[:, SPLIT:])
        pos_sb = held.tile([C, N], F32, name="pos_sb")
        w_in_sb = held.tile([C, F], BF16, name="w_in_sb")
        w_out_sb = held.tile([128, BLOCKS, C], BF16, name="w_out_sb")
        loaded = 0
        for k, width in enumerate(POS_LOADS):
            nc.sync.dma_start(pos_sb[:, loaded : loaded + width], pos[:, loaded : loaded + width])
            loaded += width
            if k == 1:
                nc.sync.dma_start(w_in_sb[:], w_in)
            if k == 3:
                nc.sync.dma_start(w_out_sb[:], w_out.rearrange("(b p) c -> p b c", p=128))

        x0 = [held.tile([C, size], F32, name=f"x0_{j}") for j, size in enumerate(PIECES)]
        x0_bf = [held.tile([C, size], BF16, name=f"x0_bf{j}") for j, size in enumerate(PIECES)]
        hidden = [held.tile([128, BLOCKS, size], BF16, name=f"hidden{j}") for j, size in enumerate(PIECES)]

        def look_up(j):
            for first in range(0, PIECES[j], LOOK):
                last = min(first + LOOK, PIECES[j])
                lo, hi = STARTS[j] + first, STARTS[j] + last
                picked = table[:].indirect(offsets[:, lo // 16 : hi // 16])
                nc.vector.tensor_tensor(x0[j][:, first:last], picked, pos_sb[:, lo:hi], ADD)
                if STARTS[j] < HEAD:
                    nc.scalar.copy(x0_bf[j][:, first:last], x0[j][:, first:last])
                else:
                    nc.vector.tensor_copy(x0_bf[j][:, first:last], x0[j][:, first:last])

        def hidden_layer(j):
            together = BLOCKS if STARTS[j] < HEAD else BLOCKS // 2
            for first in range(0, BLOCKS, together):
                hidden_ps = hidden_banks.tile([128, together, PIECES[j]], BF16, name="hidden_ps")
                for b in range(first, first + together):
                    nc.tensor.matmul(hidden_ps[:, b - first, :], w_in_sb[:, b * 128 : (b + 1) * 128], x0_bf[j][:], start=True, stop=True)
                if first > 0 and STARTS[j] >= N // 2:
                    nc.vector.tensor_scalar_max(hidden[j][:, first : first + together, :], hidden_ps[:], 0.0)
                else:
                    nc.scalar.activation(hidden[j][:, first : first + together, :], hidden_ps[:], RELU)

        def output_layer(j):
            start, size = STARTS[j], PIECES[j]
            out_ps = out_banks.tile([C, size], F32, name="out_ps")
            for b in range(BLOCKS):
                nc.tensor.matmul(out_ps[:], w_out_sb[:, b, :], hidden[j][:, b, :], start=(b == 0), stop=(b == BLOCKS - 1))
            result = held.tile([C, size], F32, name=f"result{j}")
            nc.vector.tensor_tensor(result[:], out_ps[:], x0[j][:], ADD)
            nc.sync.dma_start(out[:, start : start + size], result[:])

        for i in range(-AHEAD - LOOK_AHEAD, len(PIECES)):
            if i + AHEAD + LOOK_AHEAD < len(PIECES):
                look_up(i + AHEAD + LOOK_AHEAD)
            if 0 <= i + AHEAD < len(PIECES):
                hidden_layer(i + AHEAD)
            if i >= 0:
                output_layer(i)
